import numpy as np
import ml_dtypes


BF16 = ml_dtypes.bfloat16


def bf(x):
    return np.asarray(x, np.float32).astype(BF16)


def f64(x):
    return np.asarray(x).astype(np.float64)


E2M1 = np.array([0.0, 0.5, 1.0, 1.5, 2.0, 3.0, 4.0, 6.0, -0.0, -0.5, -1.0, -1.5, -2.0, -3.0, -4.0, -6.0])


def pack_weight(w, fmt):
    k, n = w.shape
    w = f64(bf(w)).reshape(k // 32, 32, n)
    amax = np.abs(w).max(1)
    if fmt == "e4m3":
        byte = np.frexp(amax)[1] - 1 + 127 - 7
    else:
        mant, ex = np.frexp(amax / 6.0)
        byte = np.where(mant > 0.5, ex, ex - 1) + 127
    byte = np.clip(np.where(amax > 0, byte, 1), 1, 254)
    scaled = (w * np.exp2(127.0 - byte)[:, None, :]).reshape(k, n).astype(np.float32)
    by_word = np.ascontiguousarray(scaled.reshape(k // 512, 128, 4, n).transpose(0, 1, 3, 2))
    if fmt == "e4m3":
        words = by_word.astype(ml_dtypes.float8_e4m3fn).view(np.uint8)
    else:
        c = by_word.astype(ml_dtypes.float4_e2m1fn).view(np.uint8) & 0xF
        words = c[..., 0::2] | (c[..., 1::2] << 4)
    return np.ascontiguousarray(words), np.ascontiguousarray(byte.astype(np.uint8).reshape(k // 512, 16, n))


def unpack_weight(words, scales, fmt):
    g, p, n, _ = words.shape
    if fmt == "e4m3":
        vals = np.ascontiguousarray(words).view(ml_dtypes.float8_e4m3fn).astype(np.float64)
    else:
        nib = np.empty((g, p, n, 4), np.uint8)
        nib[..., 0::2] = words & 0xF
        nib[..., 1::2] = words >> 4
        vals = E2M1[nib]
    vals = vals * np.repeat(np.exp2(scales.astype(np.float64) - 127.0), 8, axis=1)[..., None]
    return vals.transpose(0, 1, 3, 2).reshape(g * 512, n)

def pack4(w):
    words, scales = pack_weight(w, "e2m1")
    return words.reshape(words.shape[0], 128, -1), scales


def unpack4(words, scales):
    return unpack_weight(words.reshape(words.shape[0], 128, -1, 2), scales, "e2m1")


def kspread(k):
    return np.exp2(np.repeat(np.random.randint(-6, 7, k // 32), 32).astype(np.float64))


B, S, T, E, D, H = 1, 1024, 1024, 4096, 4096, 16
DK = D // H


def rope_tables(n):
    m = np.arange(n, dtype=np.float64)[:, None]
    i = np.repeat(np.arange(DK // 2, dtype=np.float64), 2)[None, :]
    ang = m * np.exp(-(2.0 * np.log(1e4) / DK) * i)
    return np.cos(ang), np.sin(ang)


def rotate_pairs(x):
    return np.stack([-x[..., 1::2], x[..., 0::2]], axis=-1).reshape(x.shape)


def setup_inputs():
    s = kspread(E)
    x = np.random.standard_normal((B, S, E)) * s
    x_words, x_scales = pack4(x.reshape(B * S, E).T)
    w_words, w_scales = pack4(np.random.standard_normal((E, D)) * 1.1 / np.sqrt(E) / s[:, None])
    b = bf(np.random.standard_normal(D) * 0.4)
    return {"x_words": x_words, "x_scales": x_scales, "w_words": w_words, "w_scales": w_scales, "b": b}


def reference(x_words, x_scales, w_words, w_scales, b):
    p = (unpack4(x_words, x_scales).T.reshape(B, S, E) @ unpack4(w_words, w_scales)) + f64(b)
    p = p.reshape(B, S, H, DK).transpose(0, 2, 1, 3)
    r1, r2 = rope_tables(S)
    return p * r1 + rotate_pairs(p) * r2

@@ -1,0 +1,273 @@
+from contextlib import ExitStack
+
+import concourse.mybir as mybir
+from concourse.masks import make_identity
+
+F32 = mybir.dt.float32
+BF16 = mybir.dt.bfloat16
+I32 = mybir.dt.int32
+U8 = mybir.dt.uint8
+FP4X4 = mybir.dt.float4_e2m1fn_x4
+ALU = mybir.AluOpType
+ACT = mybir.ActivationFunctionType
+
+P = 128
+TOKENS = 1024
+K = 4096
+CHANNELS = 4096
+HEAD = 256
+PAIRS = HEAD // 2
+PASSES = K // 512
+BLOCK = 512
+N_BLOCKS = CHANNELS // BLOCK
+T_TILES = TOKENS // P
+BANKS = N_BLOCKS * T_TILES
+HALF = 4
+ACC_BANKS = 4
+
+FLOPS = 2 * TOKENS * K * CHANNELS
+
+PI = 3.141592653589793
+TWO_PI_HI = 6.28125
+TWO_PI_LO = 2.0 * PI - TWO_PI_HI
+
+Z_AT = 516
+Z_COLS = 1032
+
+
+def tile_multiheadedattention_pa_kernel(tc, x_words, x_scales, w_words, w_scales, b, out):
+    nc = tc.nc
+
+    with ExitStack() as ctx:
+        keep = ctx.enter_context(tc.tile_pool(name="keep", bufs=1))
+        head = ctx.enter_context(tc.tile_pool(name="head", bufs=1))
+        ep = ctx.enter_context(tc.tile_pool(name="ep", bufs=4))
+        accp = ctx.enter_context(tc.psum_pool(name="accp", bufs=ACC_BANKS))
+        tabp = ctx.enter_context(tc.psum_pool(name="tabp", bufs=1))
+        ctx.enter_context(tc.manual_schedule())
+
+        xc = []
+        xp = []
+        for h in range(2):
+            xc.append(keep.tile([P, PASSES, 2 * BLOCK], U8, name="xc%d" % h, align_bytes=64))
+            xp.append(keep.tile([P, PASSES, BLOCK], U8, name="xp%d" % h, align_bytes=64))
+        wc = []
+        wp = []
+        for nb in range(N_BLOCKS):
+            wc.append(keep.tile([P, PASSES, 2 * BLOCK], U8, name="wc%d" % nb, align_bytes=64))
+            wp.append(keep.tile([P, PASSES, BLOCK], U8, name="wp%d" % nb, align_bytes=64))
+        bias = keep.tile([P, CHANNELS], BF16, name="bias")
+
+        def load_codes(dst, src, block, g0, g1):
+            nc.sync.dma_start(
+                out=dst[:, g0:g1, :].bitcast(I32),
+                in_=src[g0:g1, :, 2 * BLOCK * block : 2 * BLOCK * (block + 1)].rearrange("g p n -> p g n").bitcast(I32),
+            )
+
+        def load_scales(dst, src, block, g0, g1):
+            for q in range(4):
+                nc.sync.dma_start(
+                    out=dst[32 * q : 32 * q + 4, g0:g1, :].bitcast(I32),
+                    in_=src[g0:g1, 4 * q : 4 * q + 4, BLOCK * block : BLOCK * (block + 1)]
+                    .rearrange("g r n -> r g n")
+                    .bitcast(I32),
+                )
+
+        def load_w(nb):
+            load_codes(wc[nb], w_words, nb, 0, PASSES)
+            load_scales(wp[nb], w_scales, nb, 0, PASSES)
+
+        nc.vector.memset(xp[0][:, 0:2, :].bitcast(I32), 0)
+        nc.vector.memset(wp[0][:, 0:2, :].bitcast(I32), 0)
+        nc.vector.memset(xp[0][:, 2:PASSES, :].bitcast(I32), 0)
+        nc.vector.memset(wp[0][:, 2:PASSES, :].bitcast(I32), 0)
+
+        load_codes(xc[0], x_words, 0, 0, 1)
+        load_codes(wc[0], w_words, 0, 0, 1)
+        load_scales(xp[0], x_scales, 0, 0, 2)
+        load_scales(wp[0], w_scales, 0, 0, 2)
+        load_codes(xc[0], x_words, 0, 1, 4)
+        load_codes(wc[0], w_words, 0, 1, 4)
+        load_scales(xp[0], x_scales, 0, 2, PASSES)
+        load_scales(wp[0], w_scales, 0, 2, PASSES)
+        load_codes(xc[0], x_words, 0, 4, PASSES)
+        load_codes(wc[0], w_words, 0, 4, PASSES)
+
+        ident = head.tile([P, P], F32, name="ident")
+        make_identity(nc, ident[:])
+        pos = head.tile([P, TOKENS], F32, name="pos")
+        nc.gpsimd.iota(pos[:], pattern=[[1, TOKENS]], base=0, channel_multiplier=0, allow_small_or_imprecise_dtypes=True)
+        nc.gpsimd.memset(xp[1][:].bitcast(F32), 0.0)
+        nc.gpsimd.memset(wp[1][:].bitcast(F32), 0.0)
+
+        freq_row = head.tile([P, PAIRS], F32, name="freq_row")
+        nc.vector.memset(freq_row[:, 0:1], 1.0)
+        for s in range(7):
+            n = 2**s
+            nc.vector.tensor_scalar(
+                out=freq_row[:, n : 2 * n], in0=freq_row[:, 0:n], scalar1=10000.0 ** (-n / 128.0), scalar2=None, op0=ALU.mult
+            )
+        warm = head.tile([P, 1], F32, name="warm")
+        nc.scalar.activation(out=warm[:], in_=freq_row[:, 0:1], func=ACT.Sin)
+
+        freq_ps = tabp.tile([P, P], F32, name="freq_ps", tag="tab3")
+        nc.tensor.transpose(out=freq_ps[:], in_=freq_row[:], identity=ident[:])
+        freq = head.tile([P, 1], F32, name="freq")
+        nc.vector.tensor_copy(out=freq[:], in_=freq_ps[:, 0:1])
+
+        ang = []
+        turns = []
+        tabT = []
+        for c in range(2):
+            ang.append(head.tile([P, 2, HALF * P], F32, name="ang%d" % c))
+            turns.append(head.tile([P, 2, HALF * P], I32, name="turns%d" % c))
+            tabT.append(head.tile([P, 2, HALF * P], F32, name="tabT%d" % c))
+        for c in range(2):
+            m_cols = pos[:, HALF * P * c : HALF * P * (c + 1)]
+            nc.gpsimd.tensor_scalar(
+                out=ang[c][:, 0, :], in0=m_cols, scalar1=freq[:, 0:1], scalar2=0.0, op0=ALU.mult, op1=ALU.add
+            )
+            nc.gpsimd.tensor_scalar(
+                out=ang[c][:, 1, :], in0=m_cols, scalar1=freq[:, 0:1], scalar2=-0.5 * PI, op0=ALU.mult, op1=ALU.add
+            )
+        for nb in range(2, N_BLOCKS):
+            nc.gpsimd.memset(wp[nb][:].bitcast(F32), 0.0)
+
+        def flat(t):
+            return t[:].rearrange("p a m -> p (a m)")
+
+        def reduce_turns(c):
+            nc.vector.tensor_scalar(
+                out=flat(turns[c]), in0=flat(ang[c]), scalar1=0.5 / PI, scalar2=0.25, op0=ALU.mult, op1=ALU.add
+            )
+
+        def reduce_step(c, part):
+            nc.vector.scalar_tensor_tensor(
+                out=flat(ang[c]), in0=flat(turns[c]), scalar=-part, in1=flat(ang[c]), op0=ALU.mult, op1=ALU.add
+            )
+
+        def half_sine_squared(c):
+            nc.scalar.activation(out=flat(tabT[c]), in_=flat(ang[c]), func=ACT.Sin, scale=0.5)
+            nc.scalar.activation(out=flat(tabT[c]), in_=flat(tabT[c]), func=ACT.Square, scale=2.0**0.5)
+
+        def finish_table(c):
+            nc.vector.tensor_scalar(
+                out=flat(tabT[c]), in0=flat(tabT[c]), scalar1=-1.0, scalar2=1.0, op0=ALU.mult, op1=ALU.add
+            )
+
+        reduce_turns(0)
+        reduce_step(0, TWO_PI_HI)
+        reduce_step(0, TWO_PI_LO)
+        half_sine_squared(0)
+        reduce_turns(1)
+        reduce_step(1, TWO_PI_HI)
+        finish_table(0)
+        reduce_step(1, TWO_PI_LO)
+        half_sine_squared(1)
+
+        load_codes(xc[1], x_words, 1, 0, PASSES)
+        load_scales(xp[1], x_scales, 1, 0, PASSES)
+        nc.sync.dma_start(out=bias[:, 0:BLOCK], in_=b[0:BLOCK].partition_broadcast(P))
+        load_w(1)
+        nc.sync.dma_start(out=bias[:, BLOCK:CHANNELS], in_=b[BLOCK:CHANNELS].partition_broadcast(P))
+        load_w(2)
+
+        tab = []
+
+        def put_tables(c):
+            for u in range(2):
+                bank = tabp.tile([P, 4, P], F32, name="tab%d" % (2 * c + u), tag="tab%d" % (2 * c + u))
+                tab.append(bank)
+                for v in range(2):
+                    for a in range(2):
+                        nc.tensor.transpose(
+                            out=bank[:, 2 * v + a, :],
+                            in_=tabT[c][:, a, P * (2 * u + v) : P * (2 * u + v + 1)],
+                            identity=ident[:],
+                        )
+
+        acc = {}
+        zt = {}
+
+        def mm(j, g):
+            nb, t = divmod(j, T_TILES)
+            h, tt = divmod(t, HALF)
+            nc.tensor.matmul_mx(
+                out=acc[j][:],
+                lhsT=xc[h][:, g, 2 * P * tt : 2 * P * (tt + 1)].bitcast(FP4X4),
+                lhsT_scale=xp[h][:, g, P * tt : P * (tt + 1)],
+                rhs=wc[nb][:, g, :].bitcast(FP4X4),
+                rhs_scale=wp[nb][:, g, :],
+                start=(g == 0),
+                stop=(g == PASSES - 1),
+            )
+
+        def new_acc(j):
+            acc[j] = accp.tile([P, BLOCK], F32, name="acc", tag="acc")
+
+        def add_bias(j):
+            nb = j // T_TILES
+            z = ep.tile([P, Z_COLS], F32, name="z", tag="z", bufs=5)
+            zt[j] = z
+            nc.vector.tensor_tensor(
+                out=z[:, Z_AT : Z_AT + BLOCK], in0=acc[j][:], in1=bias[:, BLOCK * nb : BLOCK * (nb + 1)], op=ALU.add
+            )
+            nc.scalar.mul(out=z[:, 0:BLOCK], in_=z[:, Z_AT : Z_AT + BLOCK], mul=-1.0)
+
+        def spread(t, a):
+            return tab[t // 2][:, 2 * (t % 2) + a, :].unsqueeze(1).unsqueeze(3).to_broadcast([P, 2, PAIRS, 2])
+
+        def rotate(j):
+            nb, t = divmod(j, T_TILES)
+            z = zt[j]
+            zc = ep.tile([P, BLOCK], F32, name="zc", tag="zc")
+            zs = ep.tile([P, BLOCK], F32, name="zs", tag="zs")
+            res = ep.tile([P, BLOCK], F32, name="res", tag="res", bufs=6)
+            nc.vector.tensor_tensor(
+                out=zc[:].rearrange("p (h i e) -> p h i e", h=2, e=2),
+                in0=z[:, Z_AT : Z_AT + BLOCK].rearrange("p (h i e) -> p h i e", h=2, e=2),
+                in1=spread(t, 0),
+                op=ALU.mult,
+            )
+            partner = (
+                z[:, 1 : 1 + 2 * (Z_AT - 1)]
+                .rearrange("p (e w) -> p e w", e=2)[:, :, 0:BLOCK:2]
+                .rearrange("p e (h i) -> p h i e", h=2)
+            )
+            nc.vector.tensor_tensor(
+                out=zs[:].rearrange("p (h i e) -> p h i e", h=2, e=2), in0=partner, in1=spread(t, 1), op=ALU.mult
+            )
+            nc.gpsimd.tensor_tensor(out=res[:], in0=zc[:], in1=zs[:], op=ALU.add)
+            nc.sync.dma_start(
+                out=out[0, 2 * nb : 2 * nb + 2, P * t : P * (t + 1), :].rearrange("h m j -> m h j"),
+                in_=res[:].rearrange("p (h j) -> p h j", h=2),
+            )
+
+        for j in range(ACC_BANKS):
+            new_acc(j)
+        for g in range(PASSES):
+            for j in range(ACC_BANKS):
+                mm(j, g)
+        put_tables(0)
+
+        rotated = 0
+        for j in range(BANKS):
+            if j >= ACC_BANKS:
+                new_acc(j)
+                for g in range(PASSES):
+                    mm(j, g)
+            if j == 5:
+                put_tables(1)
+            add_bias(j)
+            if j == 3:
+                finish_table(1)
+            if j < 3:
+                continue
+            last = j if j >= BANKS - 2 else j - 1
+            count = 0
+            while rotated <= last and count < 2:
+                rotate(rotated)
+                if rotated % T_TILES == 1 and rotated // T_TILES + 3 < N_BLOCKS:
+                    load_w(rotated // T_TILES + 3)
+                rotated += 1
+                count += 1

@@ -22,8 +22,8 @@ BLOCK = 512
 N_BLOCKS = CHANNELS // BLOCK
 T_TILES = TOKENS // P
 BANKS = N_BLOCKS * T_TILES
-HALF = 4
 ACC_BANKS = 4
+WARM_MATMULS = 8
 
 FLOPS = 2 * TOKENS * K * CHANNELS
 
@@ -46,11 +46,8 @@ def tile_multiheadedattention_pa_kernel(tc, x_words, x_scales, w_words, w_scales
         tabp = ctx.enter_context(tc.psum_pool(name="tabp", bufs=1))
         ctx.enter_context(tc.manual_schedule())
 
-        xc = []
-        xp = []
-        for h in range(2):
-            xc.append(keep.tile([P, PASSES, 2 * BLOCK], U8, name="xc%d" % h, align_bytes=64))
-            xp.append(keep.tile([P, PASSES, BLOCK], U8, name="xp%d" % h, align_bytes=64))
+        xc = keep.tile([P, PASSES, 2 * TOKENS], U8, name="xc", align_bytes=64)
+        xp = keep.tile([P, PASSES, TOKENS], U8, name="xp", align_bytes=64)
         wc = []
         wp = []
         for nb in range(N_BLOCKS):
@@ -58,46 +55,67 @@ def tile_multiheadedattention_pa_kernel(tc, x_words, x_scales, w_words, w_scales
             wp.append(keep.tile([P, PASSES, BLOCK], U8, name="wp%d" % nb, align_bytes=64))
         bias = keep.tile([P, CHANNELS], BF16, name="bias")
 
-        def load_codes(dst, src, block, g0, g1):
+        def load_codes(dst, src, c0, c1, g0, g1):
             nc.sync.dma_start(
                 out=dst[:, g0:g1, :].bitcast(I32),
-                in_=src[g0:g1, :, 2 * BLOCK * block : 2 * BLOCK * (block + 1)].rearrange("g p n -> p g n").bitcast(I32),
+                in_=src[g0:g1, :, 2 * c0 : 2 * c1].rearrange("g p n -> p g n").bitcast(I32),
             )
 
-        def load_scales(dst, src, block, g0, g1):
+        def load_scales(dst, src, c0, c1, g0, g1):
             for q in range(4):
                 nc.sync.dma_start(
                     out=dst[32 * q : 32 * q + 4, g0:g1, :].bitcast(I32),
-                    in_=src[g0:g1, 4 * q : 4 * q + 4, BLOCK * block : BLOCK * (block + 1)]
-                    .rearrange("g r n -> r g n")
-                    .bitcast(I32),
+                    in_=src[g0:g1, 4 * q : 4 * q + 4, c0:c1].rearrange("g r n -> r g n").bitcast(I32),
                 )
 
+        def load_x_codes(g0, g1):
+            load_codes(xc, x_words, 0, TOKENS, g0, g1)
+
+        def load_w_codes(nb, g0, g1):
+            load_codes(wc[nb], w_words, BLOCK * nb, BLOCK * (nb + 1), g0, g1)
+
+        def load_x_scales(g0, g1):
+            load_scales(xp, x_scales, 0, TOKENS, g0, g1)
+
+        def load_w_scales(nb, g0, g1):
+            load_scales(wp[nb], w_scales, BLOCK * nb, BLOCK * (nb + 1), g0, g1)
+
         def load_w(nb):
-            load_codes(wc[nb], w_words, nb, 0, PASSES)
-            load_scales(wp[nb], w_scales, nb, 0, PASSES)
+            load_w_codes(nb, 0, PASSES)
+            load_w_scales(nb, 0, PASSES)
 
-        nc.vector.memset(xp[0][:, 0:2, :].bitcast(I32), 0)
-        nc.vector.memset(wp[0][:, 0:2, :].bitcast(I32), 0)
-        nc.vector.memset(xp[0][:, 2:PASSES, :].bitcast(I32), 0)
-        nc.vector.memset(wp[0][:, 2:PASSES, :].bitcast(I32), 0)
+        nc.vector.memset(xp[:, 0:1, :].bitcast(I32), 0)
+        nc.vector.memset(wp[0][:, 0:1, :].bitcast(I32), 0)
+        nc.vector.memset(xp[:, 1:PASSES, :].bitcast(I32), 0)
+        nc.vector.memset(wp[0][:, 1:PASSES, :].bitcast(I32), 0)
 
-        load_codes(xc[0], x_words, 0, 0, 1)
-        load_codes(wc[0], w_words, 0, 0, 1)
-        load_scales(xp[0], x_scales, 0, 0, 2)
-        load_scales(wp[0], w_scales, 0, 0, 2)
-        load_codes(xc[0], x_words, 0, 1, 4)
-        load_codes(wc[0], w_words, 0, 1, 4)
-        load_scales(xp[0], x_scales, 0, 2, PASSES)
-        load_scales(wp[0], w_scales, 0, 2, PASSES)
-        load_codes(xc[0], x_words, 0, 4, PASSES)
-        load_codes(wc[0], w_words, 0, 4, PASSES)
+        load_x_codes(0, 1)
+        load_w_codes(0, 0, 1)
+        load_x_scales(0, 1)
+        load_w_scales(0, 0, 1)
+        load_x_codes(1, 2)
+        load_w_codes(0, 1, 2)
+        load_x_scales(1, 4)
+        load_w_scales(0, 1, 4)
+        load_x_codes(2, 4)
+        load_w_codes(0, 2, 4)
+        load_x_codes(4, 6)
+        load_w_codes(0, 4, 6)
+        load_x_scales(4, PASSES)
+        load_w_scales(0, 4, PASSES)
+        load_x_codes(6, PASSES)
+        load_w_codes(0, 6, PASSES)
+
+        zeros = head.tile([P, BLOCK], BF16, name="zeros")
+        nc.gpsimd.memset(zeros[:], 0.0)
+        warm_ps = tabp.tile([P, BLOCK], F32, name="warm_ps", tag="tab2")
+        for r in range(WARM_MATMULS):
+            nc.tensor.matmul(out=warm_ps[:], lhsT=zeros[:, 0:P], rhs=zeros[:], start=True, stop=True)
 
         ident = head.tile([P, P], F32, name="ident")
         make_identity(nc, ident[:])
         pos = head.tile([P, TOKENS], F32, name="pos")
         nc.gpsimd.iota(pos[:], pattern=[[1, TOKENS]], base=0, channel_multiplier=0, allow_small_or_imprecise_dtypes=True)
-        nc.gpsimd.memset(xp[1][:].bitcast(F32), 0.0)
         nc.gpsimd.memset(wp[1][:].bitcast(F32), 0.0)
 
         freq_row = head.tile([P, PAIRS], F32, name="freq_row")
@@ -115,15 +133,16 @@ def tile_multiheadedattention_pa_kernel(tc, x_words, x_scales, w_words, w_scales
         freq = head.tile([P, 1], F32, name="freq")
         nc.vector.tensor_copy(out=freq[:], in_=freq_ps[:, 0:1])
 
+        half = TOKENS // 2
         ang = []
         turns = []
         tabT = []
         for c in range(2):
-            ang.append(head.tile([P, 2, HALF * P], F32, name="ang%d" % c))
-            turns.append(head.tile([P, 2, HALF * P], I32, name="turns%d" % c))
-            tabT.append(head.tile([P, 2, HALF * P], F32, name="tabT%d" % c))
+            ang.append(head.tile([P, 2, half], F32, name="ang%d" % c))
+            turns.append(head.tile([P, 2, half], I32, name="turns%d" % c))
+            tabT.append(head.tile([P, 2, half], F32, name="tabT%d" % c))
         for c in range(2):
-            m_cols = pos[:, HALF * P * c : HALF * P * (c + 1)]
+            m_cols = pos[:, half * c : half * (c + 1)]
             nc.gpsimd.tensor_scalar(
                 out=ang[c][:, 0, :], in0=m_cols, scalar1=freq[:, 0:1], scalar2=0.0, op0=ALU.mult, op1=ALU.add
             )
@@ -136,138 +155,133 @@ def tile_multiheadedattention_pa_kernel(tc, x_words, x_scales, w_words, w_scales
         def flat(t):
             return t[:].rearrange("p a m -> p (a m)")
 
-        def reduce_turns(c):
+        for c in range(2):
             nc.vector.tensor_scalar(
                 out=flat(turns[c]), in0=flat(ang[c]), scalar1=0.5 / PI, scalar2=0.25, op0=ALU.mult, op1=ALU.add
             )
-
-        def reduce_step(c, part):
-            nc.vector.scalar_tensor_tensor(
-                out=flat(ang[c]), in0=flat(turns[c]), scalar=-part, in1=flat(ang[c]), op0=ALU.mult, op1=ALU.add
-            )
-
-        def half_sine_squared(c):
+            for part in (TWO_PI_HI, TWO_PI_LO):
+                nc.vector.scalar_tensor_tensor(
+                    out=flat(ang[c]), in0=flat(turns[c]), scalar=-part, in1=flat(ang[c]), op0=ALU.mult, op1=ALU.add
+                )
             nc.scalar.activation(out=flat(tabT[c]), in_=flat(ang[c]), func=ACT.Sin, scale=0.5)
             nc.scalar.activation(out=flat(tabT[c]), in_=flat(tabT[c]), func=ACT.Square, scale=2.0**0.5)
-
-        def finish_table(c):
+        for c in range(2):
             nc.vector.tensor_scalar(
                 out=flat(tabT[c]), in0=flat(tabT[c]), scalar1=-1.0, scalar2=1.0, op0=ALU.mult, op1=ALU.add
             )
 
-        reduce_turns(0)
-        reduce_step(0, TWO_PI_HI)
-        reduce_step(0, TWO_PI_LO)
-        half_sine_squared(0)
-        reduce_turns(1)
-        reduce_step(1, TWO_PI_HI)
-        finish_table(0)
-        reduce_step(1, TWO_PI_LO)
-        half_sine_squared(1)
-
-        load_codes(xc[1], x_words, 1, 0, PASSES)
-        load_scales(xp[1], x_scales, 1, 0, PASSES)
-        nc.sync.dma_start(out=bias[:, 0:BLOCK], in_=b[0:BLOCK].partition_broadcast(P))
+        nc.sync.dma_start(out=bias[:, 0 : 2 * BLOCK], in_=b[0 : 2 * BLOCK].partition_broadcast(P))
         load_w(1)
-        nc.sync.dma_start(out=bias[:, BLOCK:CHANNELS], in_=b[BLOCK:CHANNELS].partition_broadcast(P))
         load_w(2)
+        nc.sync.dma_start(out=bias[:, 2 * BLOCK : CHANNELS], in_=b[2 * BLOCK : CHANNELS].partition_broadcast(P))
 
-        tab = []
-
-        def put_tables(c):
-            for u in range(2):
-                bank = tabp.tile([P, 4, P], F32, name="tab%d" % (2 * c + u), tag="tab%d" % (2 * c + u))
-                tab.append(bank)
-                for v in range(2):
-                    for a in range(2):
-                        nc.tensor.transpose(
-                            out=bank[:, 2 * v + a, :],
-                            in_=tabT[c][:, a, P * (2 * u + v) : P * (2 * u + v + 1)],
-                            identity=ident[:],
-                        )
-
-        acc = {}
-        zt = {}
-
-        def mm(j, g):
-            nb, t = divmod(j, T_TILES)
-            h, tt = divmod(t, HALF)
+        def mm(acc, t, c0, width, g):
+            nb, lo = divmod(c0, BLOCK)
             nc.tensor.matmul_mx(
-                out=acc[j][:],
-                lhsT=xc[h][:, g, 2 * P * tt : 2 * P * (tt + 1)].bitcast(FP4X4),
-                lhsT_scale=xp[h][:, g, P * tt : P * (tt + 1)],
-                rhs=wc[nb][:, g, :].bitcast(FP4X4),
-                rhs_scale=wp[nb][:, g, :],
+                out=acc[:],
+                lhsT=xc[:, g, 2 * P * t : 2 * P * (t + 1)].bitcast(FP4X4),
+                lhsT_scale=xp[:, g, P * t : P * (t + 1)],
+                rhs=wc[nb][:, g, 2 * lo : 2 * (lo + width)].bitcast(FP4X4),
+                rhs_scale=wp[nb][:, g, lo : lo + width],
                 start=(g == 0),
                 stop=(g == PASSES - 1),
             )
 
-        def new_acc(j):
-            acc[j] = accp.tile([P, BLOCK], F32, name="acc", tag="acc")
+        def add_bias(acc, c0, width):
+            z = ep.tile([P, Z_COLS], F32, name="z", tag="z", bufs=10)
+            nc.vector.tensor_tensor(out=z[:, Z_AT : Z_AT + width], in0=acc[:], in1=bias[:, c0 : c0 + width], op=ALU.add)
+            nc.scalar.mul(out=z[:, 0:width], in_=z[:, Z_AT : Z_AT + width], mul=-1.0)
+            return z
 
-        def add_bias(j):
-            nb = j // T_TILES
-            z = ep.tile([P, Z_COLS], F32, name="z", tag="z", bufs=5)
-            zt[j] = z
-            nc.vector.tensor_tensor(
-                out=z[:, Z_AT : Z_AT + BLOCK], in0=acc[j][:], in1=bias[:, BLOCK * nb : BLOCK * (nb + 1)], op=ALU.add
-            )
-            nc.scalar.mul(out=z[:, 0:BLOCK], in_=z[:, Z_AT : Z_AT + BLOCK], mul=-1.0)
+        tab = []
 
-        def spread(t, a):
-            return tab[t // 2][:, 2 * (t % 2) + a, :].unsqueeze(1).unsqueeze(3).to_broadcast([P, 2, PAIRS, 2])
+        def spread(t, a, heads):
+            return tab[t // 2][:, 2 * (t % 2) + a, :].unsqueeze(1).unsqueeze(3).to_broadcast([P, heads, PAIRS, 2])
 
-        def rotate(j):
-            nb, t = divmod(j, T_TILES)
-            z = zt[j]
+        def split(ap, heads):
+            return ap.rearrange("p (h i e) -> p h i e", h=heads, e=2)
+
+        def times_cos(z, t, width):
+            heads = width // HEAD
             zc = ep.tile([P, BLOCK], F32, name="zc", tag="zc")
-            zs = ep.tile([P, BLOCK], F32, name="zs", tag="zs")
-            res = ep.tile([P, BLOCK], F32, name="res", tag="res", bufs=6)
             nc.vector.tensor_tensor(
-                out=zc[:].rearrange("p (h i e) -> p h i e", h=2, e=2),
-                in0=z[:, Z_AT : Z_AT + BLOCK].rearrange("p (h i e) -> p h i e", h=2, e=2),
-                in1=spread(t, 0),
+                out=split(zc[:, 0:width], heads),
+                in0=split(z[:, Z_AT : Z_AT + width], heads),
+                in1=spread(t, 0, heads),
                 op=ALU.mult,
             )
+            return zc
+
+        def times_sin_add_store(z, zc, t, c0, width, add_engine):
+            heads = width // HEAD
+            zs = ep.tile([P, BLOCK], F32, name="zs", tag="zs")
+            res = ep.tile([P, BLOCK], F32, name="res", tag="res", bufs=6)
             partner = (
                 z[:, 1 : 1 + 2 * (Z_AT - 1)]
-                .rearrange("p (e w) -> p e w", e=2)[:, :, 0:BLOCK:2]
-                .rearrange("p e (h i) -> p h i e", h=2)
+                .rearrange("p (e w) -> p e w", e=2)[:, :, 0:width:2]
+                .rearrange("p e (h i) -> p h i e", h=heads)
             )
-            nc.vector.tensor_tensor(
-                out=zs[:].rearrange("p (h i e) -> p h i e", h=2, e=2), in0=partner, in1=spread(t, 1), op=ALU.mult
-            )
-            nc.gpsimd.tensor_tensor(out=res[:], in0=zc[:], in1=zs[:], op=ALU.add)
+            nc.vector.tensor_tensor(out=split(zs[:, 0:width], heads), in0=partner, in1=spread(t, 1, heads), op=ALU.mult)
+            add_engine.tensor_tensor(out=res[:, 0:width], in0=zc[:, 0:width], in1=zs[:, 0:width], op=ALU.add)
+            h0 = c0 // HEAD
             nc.sync.dma_start(
-                out=out[0, 2 * nb : 2 * nb + 2, P * t : P * (t + 1), :].rearrange("h m j -> m h j"),
-                in_=res[:].rearrange("p (h j) -> p h j", h=2),
+                out=out[0, h0 : h0 + heads, P * t : P * (t + 1), :].rearrange("h m j -> m h j"),
+                in_=res[:, 0:width].rearrange("p (h j) -> p h j", h=heads),
             )
 
-        for j in range(ACC_BANKS):
-            new_acc(j)
-        for g in range(PASSES):
-            for j in range(ACC_BANKS):
-                mm(j, g)
-        put_tables(0)
+        units = []
+        for j in range(BANKS - 1):
+            units.append((j % T_TILES, BLOCK * (j // T_TILES), BLOCK))
+        units.append((T_TILES - 1, CHANNELS - 2 * HEAD, HEAD))
+        units.append((T_TILES - 1, CHANNELS - HEAD, HEAD))
+        n_units = len(units)
 
-        rotated = 0
-        for j in range(BANKS):
-            if j >= ACC_BANKS:
-                new_acc(j)
+        first = []
+        for j in range(T_TILES):
+            if j < 4:
+                first.append(tabp.tile([P, BLOCK], F32, name="first%d" % j, tag="tab%d" % j))
+            else:
+                first.append(accp.tile([P, BLOCK], F32, name="acc", tag="acc"))
+        for g in range(PASSES):
+            for j in range(T_TILES):
+                mm(first[j], units[j][0], units[j][1], BLOCK, g)
+        zq = []
+        for j in range(T_TILES):
+            zq.append(add_bias(first[j], units[j][1], BLOCK))
+
+        for u in range(4):
+            bank = tabp.tile([P, 4, P], F32, name="tab%d" % u, tag="tab%d" % u)
+            tab.append(bank)
+            for v in range(2):
+                for a in range(2):
+                    t = 2 * u + v
+                    nc.tensor.transpose(
+                        out=bank[:, 2 * v + a, :],
+                        in_=tabT[t // 4][:, a, P * (t % 4) : P * (t % 4 + 1)],
+                        identity=ident[:],
+                    )
+
+        zcq = [times_cos(zq[0], units[0][0], units[0][2])]
+        done = 0
+        for j in range(T_TILES - 1, n_units):
+            if j >= T_TILES:
+                t, c0, width = units[j]
+                acc = accp.tile([P, width], F32, name="acc", tag="acc")
                 for g in range(PASSES):
-                    mm(j, g)
-            if j == 5:
-                put_tables(1)
-            add_bias(j)
-            if j == 3:
-                finish_table(1)
-            if j < 3:
-                continue
-            last = j if j >= BANKS - 2 else j - 1
+                    mm(acc, t, c0, width, g)
+                zq.append(add_bias(acc, c0, width))
+            most = 2 if j % 2 == 1 else 1
+            if j == n_units - 1:
+                most = n_units
             count = 0
-            while rotated <= last and count < 2:
-                rotate(rotated)
-                if rotated % T_TILES == 1 and rotated // T_TILES + 3 < N_BLOCKS:
-                    load_w(rotated // T_TILES + 3)
-                rotated += 1
+            while done < min(j + 1, n_units) and count < most and (done < j or j == n_units - 1):
+                t, c0, width = units[done]
+                times_sin_add_store(
+                    zq[done], zcq[done], t, c0, width, nc.vector if done == n_units - 1 else nc.gpsimd
+                )
+                if t == 1 and c0 % BLOCK == 0 and c0 // BLOCK + 3 < N_BLOCKS:
+                    load_w(c0 // BLOCK + 3)
+                done += 1
                 count += 1
+                if done < n_units:
+                    zcq.append(times_cos(zq[done], units[done][0], units[done][2]))

@@ -249,7 +249,7 @@ def tile_multiheadedattention_pa_kernel(tc, x_words, x_scales, w_words, w_scales
         for j in range(T_TILES):
             zq.append(add_bias(first[j], units[j][1], BLOCK))
 
-        for u in range(4):
+        def put_tables(u):
             bank = tabp.tile([P, 4, P], F32, name="tab%d" % u, tag="tab%d" % u)
             tab.append(bank)
             for v in range(2):
@@ -261,6 +261,9 @@ def tile_multiheadedattention_pa_kernel(tc, x_words, x_scales, w_words, w_scales
                         identity=ident[:],
                     )
 
+        put_tables(0)
+        put_tables(1)
+
         zcq = [times_cos(zq[0], units[0][0], units[0][2])]
         done = 0
         for j in range(T_TILES - 1, n_units):
@@ -269,6 +272,9 @@ def tile_multiheadedattention_pa_kernel(tc, x_words, x_scales, w_words, w_scales
                 acc = accp.tile([P, width], F32, name="acc", tag="acc")
                 for g in range(PASSES):
                     mm(acc, t, c0, width, g)
+                if j == T_TILES:
+                    put_tables(2)
+                    put_tables(3)
                 zq.append(add_bias(acc, c0, width))
             most = 2 if j % 2 == 1 else 1
             if j == n_units - 1:

@@ -62,10 +62,10 @@ def tile_multiheadedattention_pa_kernel(tc, x_words, x_scales, w_words, w_scales
             )
 
         def load_scales(dst, src, c0, c1, g0, g1):
-            for q in range(4):
+            for r in range(4):
                 nc.sync.dma_start(
-                    out=dst[32 * q : 32 * q + 4, g0:g1, :].bitcast(I32),
-                    in_=src[g0:g1, 4 * q : 4 * q + 4, c0:c1].rearrange("g r n -> r g n").bitcast(I32),
+                    out=dst[r:P:32, g0:g1, :].bitcast(I32),
+                    in_=src[g0:g1, r:16:4, c0:c1].rearrange("g q n -> q g n").bitcast(I32),
                 )
 
         def load_x_codes(g0, g1):
@@ -249,7 +249,7 @@ def tile_multiheadedattention_pa_kernel(tc, x_words, x_scales, w_words, w_scales
         for j in range(T_TILES):
             zq.append(add_bias(first[j], units[j][1], BLOCK))
 
-        def put_tables(u):
+        for u in range(4):
             bank = tabp.tile([P, 4, P], F32, name="tab%d" % u, tag="tab%d" % u)
             tab.append(bank)
             for v in range(2):
@@ -261,9 +261,6 @@ def tile_multiheadedattention_pa_kernel(tc, x_words, x_scales, w_words, w_scales
                         identity=ident[:],
                     )
 
-        put_tables(0)
-        put_tables(1)
-
         zcq = [times_cos(zq[0], units[0][0], units[0][2])]
         done = 0
         for j in range(T_TILES - 1, n_units):
@@ -272,9 +269,6 @@ def tile_multiheadedattention_pa_kernel(tc, x_words, x_scales, w_words, w_scales
                 acc = accp.tile([P, width], F32, name="acc", tag="acc")
                 for g in range(PASSES):
                     mm(acc, t, c0, width, g)
-                if j == T_TILES:
-                    put_tables(2)
-                    put_tables(3)
                 zq.append(add_bias(acc, c0, width))
             most = 2 if j % 2 == 1 else 1
             if j == n_units - 1:

@@ -23,7 +23,7 @@ N_BLOCKS = CHANNELS // BLOCK
 T_TILES = TOKENS // P
 BANKS = N_BLOCKS * T_TILES
 ACC_BANKS = 4
-WARM_MATMULS = 8
+WARM_MATMULS = 10
 
 FLOPS = 2 * TOKENS * K * CHANNELS
 
@@ -62,10 +62,10 @@ def tile_multiheadedattention_pa_kernel(tc, x_words, x_scales, w_words, w_scales
             )
 
         def load_scales(dst, src, c0, c1, g0, g1):
-            for r in range(4):
+            for q in (0, 2, 1, 3):
                 nc.sync.dma_start(
-                    out=dst[r:P:32, g0:g1, :].bitcast(I32),
-                    in_=src[g0:g1, r:16:4, c0:c1].rearrange("g q n -> q g n").bitcast(I32),
+                    out=dst[32 * q : 32 * q + 4, g0:g1, :].bitcast(I32),
+                    in_=src[g0:g1, 4 * q : 4 * q + 4, c0:c1].rearrange("g r n -> r g n").bitcast(I32),
                 )
 
         def load_x_codes(g0, g1):
@@ -84,8 +84,8 @@ def tile_multiheadedattention_pa_kernel(tc, x_words, x_scales, w_words, w_scales
             load_w_codes(nb, 0, PASSES)
             load_w_scales(nb, 0, PASSES)
 
-        nc.vector.memset(xp[:, 0:1, :].bitcast(I32), 0)
-        nc.vector.memset(wp[0][:, 0:1, :].bitcast(I32), 0)
+        nc.gpsimd.memset(xp[:, 0:1, :].bitcast(F32), 0.0)
+        nc.gpsimd.memset(wp[0][:, 0:1, :].bitcast(F32), 0.0)
         nc.vector.memset(xp[:, 1:PASSES, :].bitcast(I32), 0)
         nc.vector.memset(wp[0][:, 1:PASSES, :].bitcast(I32), 0)
 

from contextlib import ExitStack

import concourse.mybir as mybir
from concourse.masks import make_identity

F32 = mybir.dt.float32
BF16 = mybir.dt.bfloat16
I32 = mybir.dt.int32
U8 = mybir.dt.uint8
FP4X4 = mybir.dt.float4_e2m1fn_x4
ALU = mybir.AluOpType
ACT = mybir.ActivationFunctionType

P = 128
TOKENS = 1024
K = 4096
CHANNELS = 4096
HEAD = 256
PAIRS = HEAD // 2
PASSES = K // 512
BLOCK = 512
N_BLOCKS = CHANNELS // BLOCK
T_TILES = TOKENS // P
BANKS = N_BLOCKS * T_TILES
ACC_BANKS = 4
WARM_MATMULS = 10

FLOPS = 2 * TOKENS * K * CHANNELS

PI = 3.141592653589793
TWO_PI_HI = 6.28125
TWO_PI_LO = 2.0 * PI - TWO_PI_HI

Z_AT = 516
Z_COLS = 1032


def tile_multiheadedattention_pa_kernel(tc, x_words, x_scales, w_words, w_scales, b, out):
    nc = tc.nc

    with ExitStack() as ctx:
        keep = ctx.enter_context(tc.tile_pool(name="keep", bufs=1))
        head = ctx.enter_context(tc.tile_pool(name="head", bufs=1))
        ep = ctx.enter_context(tc.tile_pool(name="ep", bufs=4))
        accp = ctx.enter_context(tc.psum_pool(name="accp", bufs=ACC_BANKS))
        tabp = ctx.enter_context(tc.psum_pool(name="tabp", bufs=1))
        ctx.enter_context(tc.manual_schedule())

        xc = keep.tile([P, PASSES, 2 * TOKENS], U8, name="xc", align_bytes=64)
        xp = keep.tile([P, PASSES, TOKENS], U8, name="xp", align_bytes=64)
        wc = []
        wp = []
        for nb in range(N_BLOCKS):
            wc.append(keep.tile([P, PASSES, 2 * BLOCK], U8, name="wc%d" % nb, align_bytes=64))
            wp.append(keep.tile([P, PASSES, BLOCK], U8, name="wp%d" % nb, align_bytes=64))
        bias = keep.tile([P, CHANNELS], BF16, name="bias")

        def load_codes(dst, src, c0, c1, g0, g1):
            nc.sync.dma_start(
                out=dst[:, g0:g1, :].bitcast(I32),
                in_=src[g0:g1, :, 2 * c0 : 2 * c1].rearrange("g p n -> p g n").bitcast(I32),
            )

        def load_scales(dst, src, c0, c1, g0, g1):
            for q in (0, 2, 1, 3):
                nc.sync.dma_start(
                    out=dst[32 * q : 32 * q + 4, g0:g1, :].bitcast(I32),
                    in_=src[g0:g1, 4 * q : 4 * q + 4, c0:c1].rearrange("g r n -> r g n").bitcast(I32),
                )

        def load_x_codes(g0, g1):
            load_codes(xc, x_words, 0, TOKENS, g0, g1)

        def load_w_codes(nb, g0, g1):
            load_codes(wc[nb], w_words, BLOCK * nb, BLOCK * (nb + 1), g0, g1)

        def load_x_scales(g0, g1):
            load_scales(xp, x_scales, 0, TOKENS, g0, g1)

        def load_w_scales(nb, g0, g1):
            load_scales(wp[nb], w_scales, BLOCK * nb, BLOCK * (nb + 1), g0, g1)

        def load_w(nb):
            load_w_codes(nb, 0, PASSES)
            load_w_scales(nb, 0, PASSES)

        nc.gpsimd.memset(xp[:, 0:1, :].bitcast(F32), 0.0)
        nc.gpsimd.memset(wp[0][:, 0:1, :].bitcast(F32), 0.0)
        nc.vector.memset(xp[:, 1:PASSES, :].bitcast(I32), 0)
        nc.vector.memset(wp[0][:, 1:PASSES, :].bitcast(I32), 0)

        load_x_codes(0, 1)
        load_w_codes(0, 0, 1)
        load_x_scales(0, 1)
        load_w_scales(0, 0, 1)
        load_x_codes(1, 2)
        load_w_codes(0, 1, 2)
        load_x_scales(1, 4)
        load_w_scales(0, 1, 4)
        load_x_codes(2, 4)
        load_w_codes(0, 2, 4)
        load_x_codes(4, 6)
        load_w_codes(0, 4, 6)
        load_x_scales(4, PASSES)
        load_w_scales(0, 4, PASSES)
        load_x_codes(6, PASSES)
        load_w_codes(0, 6, PASSES)

        zeros = head.tile([P, BLOCK], BF16, name="zeros")
        nc.gpsimd.memset(zeros[:], 0.0)
        warm_ps = tabp.tile([P, BLOCK], F32, name="warm_ps", tag="tab2")
        for r in range(WARM_MATMULS):
            nc.tensor.matmul(out=warm_ps[:], lhsT=zeros[:, 0:P], rhs=zeros[:], start=True, stop=True)

        ident = head.tile([P, P], F32, name="ident")
        make_identity(nc, ident[:])
        pos = head.tile([P, TOKENS], F32, name="pos")
        nc.gpsimd.iota(pos[:], pattern=[[1, TOKENS]], base=0, channel_multiplier=0, allow_small_or_imprecise_dtypes=True)
        nc.gpsimd.memset(wp[1][:].bitcast(F32), 0.0)

        freq_row = head.tile([P, PAIRS], F32, name="freq_row")
        nc.vector.memset(freq_row[:, 0:1], 1.0)
        for s in range(7):
            n = 2**s
            nc.vector.tensor_scalar(
                out=freq_row[:, n : 2 * n], in0=freq_row[:, 0:n], scalar1=10000.0 ** (-n / 128.0), scalar2=None, op0=ALU.mult
            )
        warm = head.tile([P, 1], F32, name="warm")
        nc.scalar.activation(out=warm[:], in_=freq_row[:, 0:1], func=ACT.Sin)

        freq_ps = tabp.tile([P, P], F32, name="freq_ps", tag="tab3")
        nc.tensor.transpose(out=freq_ps[:], in_=freq_row[:], identity=ident[:])
        freq = head.tile([P, 1], F32, name="freq")
        nc.vector.tensor_copy(out=freq[:], in_=freq_ps[:, 0:1])

        half = TOKENS // 2
        ang = []
        turns = []
        tabT = []
        for c in range(2):
            ang.append(head.tile([P, 2, half], F32, name="ang%d" % c))
            turns.append(head.tile([P, 2, half], I32, name="turns%d" % c))
            tabT.append(head.tile([P, 2, half], F32, name="tabT%d" % c))
        for c in range(2):
            m_cols = pos[:, half * c : half * (c + 1)]
            nc.gpsimd.tensor_scalar(
                out=ang[c][:, 0, :], in0=m_cols, scalar1=freq[:, 0:1], scalar2=0.0, op0=ALU.mult, op1=ALU.add
            )
            nc.gpsimd.tensor_scalar(
                out=ang[c][:, 1, :], in0=m_cols, scalar1=freq[:, 0:1], scalar2=-0.5 * PI, op0=ALU.mult, op1=ALU.add
            )
        for nb in range(2, N_BLOCKS):
            nc.gpsimd.memset(wp[nb][:].bitcast(F32), 0.0)

        def flat(t):
            return t[:].rearrange("p a m -> p (a m)")

        for c in range(2):
            nc.vector.tensor_scalar(
                out=flat(turns[c]), in0=flat(ang[c]), scalar1=0.5 / PI, scalar2=0.25, op0=ALU.mult, op1=ALU.add
            )
            for part in (TWO_PI_HI, TWO_PI_LO):
                nc.vector.scalar_tensor_tensor(
                    out=flat(ang[c]), in0=flat(turns[c]), scalar=-part, in1=flat(ang[c]), op0=ALU.mult, op1=ALU.add
                )
            nc.scalar.activation(out=flat(tabT[c]), in_=flat(ang[c]), func=ACT.Sin, scale=0.5)
            nc.scalar.activation(out=flat(tabT[c]), in_=flat(tabT[c]), func=ACT.Square, scale=2.0**0.5)
        for c in range(2):
            nc.vector.tensor_scalar(
                out=flat(tabT[c]), in0=flat(tabT[c]), scalar1=-1.0, scalar2=1.0, op0=ALU.mult, op1=ALU.add
            )

        nc.sync.dma_start(out=bias[:, 0 : 2 * BLOCK], in_=b[0 : 2 * BLOCK].partition_broadcast(P))
        load_w(1)
        load_w(2)
        nc.sync.dma_start(out=bias[:, 2 * BLOCK : CHANNELS], in_=b[2 * BLOCK : CHANNELS].partition_broadcast(P))

        def mm(acc, t, c0, width, g):
            nb, lo = divmod(c0, BLOCK)
            nc.tensor.matmul_mx(
                out=acc[:],
                lhsT=xc[:, g, 2 * P * t : 2 * P * (t + 1)].bitcast(FP4X4),
                lhsT_scale=xp[:, g, P * t : P * (t + 1)],
                rhs=wc[nb][:, g, 2 * lo : 2 * (lo + width)].bitcast(FP4X4),
                rhs_scale=wp[nb][:, g, lo : lo + width],
                start=(g == 0),
                stop=(g == PASSES - 1),
            )

        def add_bias(acc, c0, width):
            z = ep.tile([P, Z_COLS], F32, name="z", tag="z", bufs=10)
            nc.vector.tensor_tensor(out=z[:, Z_AT : Z_AT + width], in0=acc[:], in1=bias[:, c0 : c0 + width], op=ALU.add)
            nc.scalar.mul(out=z[:, 0:width], in_=z[:, Z_AT : Z_AT + width], mul=-1.0)
            return z

        tab = []

        def spread(t, a, heads):
            return tab[t // 2][:, 2 * (t % 2) + a, :].unsqueeze(1).unsqueeze(3).to_broadcast([P, heads, PAIRS, 2])

        def split(ap, heads):
            return ap.rearrange("p (h i e) -> p h i e", h=heads, e=2)

        def times_cos(z, t, width):
            heads = width // HEAD
            zc = ep.tile([P, BLOCK], F32, name="zc", tag="zc")
            nc.vector.tensor_tensor(
                out=split(zc[:, 0:width], heads),
                in0=split(z[:, Z_AT : Z_AT + width], heads),
                in1=spread(t, 0, heads),
                op=ALU.mult,
            )
            return zc

        def times_sin_add_store(z, zc, t, c0, width, add_engine):
            heads = width // HEAD
            zs = ep.tile([P, BLOCK], F32, name="zs", tag="zs")
            res = ep.tile([P, BLOCK], F32, name="res", tag="res", bufs=6)
            partner = (
                z[:, 1 : 1 + 2 * (Z_AT - 1)]
                .rearrange("p (e w) -> p e w", e=2)[:, :, 0:width:2]
                .rearrange("p e (h i) -> p h i e", h=heads)
            )
            nc.vector.tensor_tensor(out=split(zs[:, 0:width], heads), in0=partner, in1=spread(t, 1, heads), op=ALU.mult)
            add_engine.tensor_tensor(out=res[:, 0:width], in0=zc[:, 0:width], in1=zs[:, 0:width], op=ALU.add)
            h0 = c0 // HEAD
            nc.sync.dma_start(
                out=out[0, h0 : h0 + heads, P * t : P * (t + 1), :].rearrange("h m j -> m h j"),
                in_=res[:, 0:width].rearrange("p (h j) -> p h j", h=heads),
            )

        units = []
        for j in range(BANKS - 1):
            units.append((j % T_TILES, BLOCK * (j // T_TILES), BLOCK))
        units.append((T_TILES - 1, CHANNELS - 2 * HEAD, HEAD))
        units.append((T_TILES - 1, CHANNELS - HEAD, HEAD))
        n_units = len(units)

        first = []
        for j in range(T_TILES):
            if j < 4:
                first.append(tabp.tile([P, BLOCK], F32, name="first%d" % j, tag="tab%d" % j))
            else:
                first.append(accp.tile([P, BLOCK], F32, name="acc", tag="acc"))
        for g in range(PASSES):
            for j in range(T_TILES):
                mm(first[j], units[j][0], units[j][1], BLOCK, g)
        zq = []
        for j in range(T_TILES):
            zq.append(add_bias(first[j], units[j][1], BLOCK))

        for u in range(4):
            bank = tabp.tile([P, 4, P], F32, name="tab%d" % u, tag="tab%d" % u)
            tab.append(bank)
            for v in range(2):
                for a in range(2):
                    t = 2 * u + v
                    nc.tensor.transpose(
                        out=bank[:, 2 * v + a, :],
                        in_=tabT[t // 4][:, a, P * (t % 4) : P * (t % 4 + 1)],
                        identity=ident[:],
                    )

        zcq = [times_cos(zq[0], units[0][0], units[0][2])]
        done = 0
        for j in range(T_TILES - 1, n_units):
            if j >= T_TILES:
                t, c0, width = units[j]
                acc = accp.tile([P, width], F32, name="acc", tag="acc")
                for g in range(PASSES):
                    mm(acc, t, c0, width, g)
                zq.append(add_bias(acc, c0, width))
            most = 2 if j % 2 == 1 else 1
            if j == n_units - 1:
                most = n_units
            count = 0
            while done < min(j + 1, n_units) and count < most and (done < j or j == n_units - 1):
                t, c0, width = units[done]
                times_sin_add_store(
                    zq[done], zcq[done], t, c0, width, nc.vector if done == n_units - 1 else nc.gpsimd
                )
                if t == 1 and c0 % BLOCK == 0 and c0 // BLOCK + 3 < N_BLOCKS:
                    load_w(c0 // BLOCK + 3)
                done += 1
                count += 1
                if done < n_units:
                    zcq.append(times_cos(zq[done], units[done][0], units[done][2]))
